import numpy as np
import ml_dtypes


BF16 = ml_dtypes.bfloat16


def bf(x):
    return np.asarray(x, np.float32).astype(BF16)


def f64(x):
    return np.asarray(x).astype(np.float64)


E2M1 = np.array([0.0, 0.5, 1.0, 1.5, 2.0, 3.0, 4.0, 6.0, -0.0, -0.5, -1.0, -1.5, -2.0, -3.0, -4.0, -6.0])


def pack_weight(w, fmt):
    k, n = w.shape
    w = f64(bf(w)).reshape(k // 32, 32, n)
    amax = np.abs(w).max(1)
    if fmt == "e4m3":
        byte = np.frexp(amax)[1] - 1 + 127 - 7
    else:
        mant, ex = np.frexp(amax / 6.0)
        byte = np.where(mant > 0.5, ex, ex - 1) + 127
    byte = np.clip(np.where(amax > 0, byte, 1), 1, 254)
    scaled = (w * np.exp2(127.0 - byte)[:, None, :]).reshape(k, n).astype(np.float32)
    by_word = np.ascontiguousarray(scaled.reshape(k // 512, 128, 4, n).transpose(0, 1, 3, 2))
    if fmt == "e4m3":
        words = by_word.astype(ml_dtypes.float8_e4m3fn).view(np.uint8)
    else:
        c = by_word.astype(ml_dtypes.float4_e2m1fn).view(np.uint8) & 0xF
        words = c[..., 0::2] | (c[..., 1::2] << 4)
    return np.ascontiguousarray(words), np.ascontiguousarray(byte.astype(np.uint8).reshape(k // 512, 16, n))


def unpack_weight(words, scales, fmt):
    g, p, n, _ = words.shape
    if fmt == "e4m3":
        vals = np.ascontiguousarray(words).view(ml_dtypes.float8_e4m3fn).astype(np.float64)
    else:
        nib = np.empty((g, p, n, 4), np.uint8)
        nib[..., 0::2] = words & 0xF
        nib[..., 1::2] = words >> 4
        vals = E2M1[nib]
    vals = vals * np.repeat(np.exp2(scales.astype(np.float64) - 127.0), 8, axis=1)[..., None]
    return vals.transpose(0, 1, 3, 2).reshape(g * 512, n)

def pack4(w):
    words, scales = pack_weight(w, "e2m1")
    return words.reshape(words.shape[0], 128, -1), scales


def unpack4(words, scales):
    return unpack_weight(words.reshape(words.shape[0], 128, -1, 2), scales, "e2m1")


def kspread(k):
    return np.exp2(np.repeat(np.random.randint(-6, 7, k // 32), 32).astype(np.float64))


B, N, D, L = 1, 512, 4096, 256
SEGS = N // L


def setup_inputs():
    s = kspread(D)
    col = np.concatenate([np.full(D, np.sqrt(SEGS)), np.ones(D)])
    x = np.random.standard_normal((B, N, D)) * s
    x_words, x_scales = pack4(np.ascontiguousarray(x.reshape(B * N, D).T))
    words, scales = pack4(np.random.standard_normal((D, D + D)) * col / np.sqrt(D) / s[:, None])
    return {"x_words": x_words, "x_scales": x_scales, "w_kv_words": words, "w_kv_scales": scales}


def reference(x_words, x_scales, w_kv_words, w_kv_scales):
    kv = unpack4(x_words, x_scales).T.reshape(B, N, D) @ unpack4(w_kv_words, w_kv_scales)
    k, v = kv[..., :D], kv[..., D:]
    keys_lm = k.reshape(B, L, SEGS, D).mean(axis=2)
    vals_lm = v.reshape(B, L, SEGS, D).mean(axis=2)
    return v, keys_lm, vals_lm

@@ -1,0 +1,207 @@
+from contextlib import ExitStack
+
+import concourse.mybir as mybir
+
+FLOPS = 2 * 512 * 4096 * 8192
+
+F32 = mybir.dt.float32
+BF16 = mybir.dt.bfloat16
+I32 = mybir.dt.int32
+U8 = mybir.dt.uint8
+FP4X4 = mybir.dt.float4_e2m1fn_x4
+ACT = mybir.ActivationFunctionType
+ALU = mybir.AluOpType
+
+P = 128
+G = 8
+NB = 512
+QB = 4
+XW = 1024
+XS = 512
+WW = QB * NB * 2
+WS = QB * NB
+WARM = 8
+
+
+def tile_ammattention_pa_kernel(tc, x_words, x_scales, w_kv_words, w_kv_scales, out_0, out_1, out_2):
+    nc = tc.nc
+    with ExitStack() as ctx:
+        keep = ctx.enter_context(tc.tile_pool(name="keep", bufs=1))
+        stage = ctx.enter_context(tc.tile_pool(name="stage", bufs=3))
+        psum = ctx.enter_context(tc.psum_pool(name="psum", bufs=1))
+        ctx.enter_context(tc.manual_schedule())
+
+        xw_raw = keep.tile([P, G * XW], U8, name="xw_raw", align_bytes=256)
+        xs_raw = keep.tile([P, G * XS], U8, name="xs_raw", align_bytes=256)
+        xw = keep.tile([P, G * XW], U8, name="xw", align_bytes=256)
+        xs = keep.tile([P, G * XS], U8, name="xs", align_bytes=256)
+        ww = []
+        wp = []
+        for s in range(3):
+            ww_s = keep.tile([P, G * WW], U8, name="ww%d" % s, align_bytes=256)
+            wp_s = keep.tile([P, G * WS], U8, name="wp%d" % s, align_bytes=256)
+            ww.append(ww_s)
+            wp.append(wp_s)
+        zeros = keep.tile([P, NB], BF16, name="zeros", align_bytes=256)
+        banks = []
+        for b in range(8):
+            bank_b = psum.tile([P, NB], F32, name="bank%d" % b)
+            banks.append(bank_b)
+
+        v_view = out_0.rearrange("b (j l two) c -> (b j) l two c", l=P, two=2)
+
+        def zero(t, lo, hi):
+            nc.vector.memset(t[:, lo:hi].bitcast(I32), 0)
+
+        def load_x_words(g0, g1):
+            nc.sync.dma_start(
+                out=xw_raw[:, g0 * XW : g1 * XW].rearrange("p (g n) -> p g n", g=g1 - g0).bitcast(I32),
+                in_=x_words[g0:g1].rearrange("g p n -> p g n").bitcast(I32),
+            )
+
+        def load_x_scales(g0, g1):
+            for q in range(4):
+                nc.sync.dma_start(
+                    out=xs_raw[32 * q : 32 * q + 4, g0 * XS : g1 * XS].rearrange("p (g n) -> p g n", g=g1 - g0).bitcast(I32),
+                    in_=x_scales[g0:g1, 4 * q : 4 * q + 4, :].rearrange("g r n -> r g n").bitcast(I32),
+                )
+
+        def load_w_words(quad, slot, g0, g1):
+            nc.sync.dma_start(
+                out=ww[slot][:, g0 * WW : g1 * WW].rearrange("p (g n) -> p g n", g=g1 - g0).bitcast(I32),
+                in_=w_kv_words[g0:g1, :, quad * WW : (quad + 1) * WW].rearrange("g p n -> p g n").bitcast(I32),
+            )
+
+        def load_w_scales(quad, slot, g0, g1):
+            for q in range(4):
+                nc.sync.dma_start(
+                    out=wp[slot][32 * q : 32 * q + 4, g0 * WS : g1 * WS].rearrange("p (g n) -> p g n", g=g1 - g0).bitcast(I32),
+                    in_=w_kv_scales[g0:g1, 4 * q : 4 * q + 4, quad * WS : (quad + 1) * WS].rearrange("g r n -> r g n").bitcast(I32),
+                )
+
+        def split_x(g, pieces):
+            w_in = xw_raw[:, g * XW : (g + 1) * XW].rearrange("p (l par b) -> p par l b", par=2, b=2)
+            w_out = xw[:, g * XW : (g + 1) * XW].rearrange("p (par l b) -> p par l b", par=2, b=2)
+            s_in = xs_raw[:, g * XS : (g + 1) * XS].rearrange("p (l par) -> p par l", par=2)
+            s_out = xs[:, g * XS : (g + 1) * XS].rearrange("p (par l) -> p par l", par=2)
+            if pieces:
+                for half in range(2):
+                    for par in range(2):
+                        rows = slice(half * P, (half + 1) * P)
+                        nc.vector.tensor_copy(out=w_out[:, par, rows, :], in_=w_in[:, par, rows, :])
+                        nc.vector.tensor_copy(out=s_out[:, par, rows], in_=s_in[:, par, rows])
+            else:
+                nc.vector.tensor_copy(out=w_out, in_=w_in)
+                nc.vector.tensor_copy(out=s_out, in_=s_in)
+
+        def mm(bank, g, par, half, slot, c, start, stop):
+            xo = g * XW + par * 512 + half * 256
+            so = g * XS + par * 256 + half * 128
+            nc.tensor.matmul_mx(
+                out=bank[:],
+                lhsT=xw[:, xo : xo + 256].bitcast(FP4X4),
+                lhsT_scale=xs[:, so : so + 128],
+                rhs=ww[slot][:, g * WW + c * 2 * NB : g * WW + (c + 1) * 2 * NB].bitcast(FP4X4),
+                rhs_scale=wp[slot][:, g * WS + c * NB : g * WS + (c + 1) * NB],
+                start=start,
+                stop=stop,
+            )
+
+        def keys_out(bank, col0, half, on_scalar, queue):
+            kl = stage.tile([P, NB], F32, name="kl", tag="kl", bufs=4)
+            if on_scalar:
+                nc.scalar.activation(out=kl[:], in_=bank[:], func=ACT.Copy, scale=0.5)
+            else:
+                nc.vector.tensor_scalar_mul(out=kl[:], in0=bank[:], scalar1=0.5)
+            queue.dma_start(out=out_1[0, half * P : (half + 1) * P, col0 : col0 + NB], in_=kl[:])
+
+        def values_out(bank_e, bank_o, col0, half):
+            vt = stage.tile([P, 2, NB], F32, name="vt", tag="vt", bufs=3)
+            he = stage.tile([P, NB], F32, name="he", tag="he", bufs=2)
+            lm = stage.tile([P, NB], F32, name="lm", tag="lm", bufs=3)
+            nc.scalar.copy(out=vt[:, 0, :], in_=bank_e[:])
+            nc.scalar.activation(out=he[:], in_=bank_e[:], func=ACT.Copy, scale=0.5)
+            nc.vector.tensor_copy(out=vt[:, 1, :], in_=bank_o[:])
+            nc.vector.scalar_tensor_tensor(out=lm[:], in0=bank_o[:], scalar=0.5, in1=he[:], op0=ALU.mult, op1=ALU.add)
+            nc.gpsimd.dma_start(out=v_view[half, :, :, col0 : col0 + NB], in_=vt[:])
+            nc.gpsimd.dma_start(out=out_2[0, half * P : (half + 1) * P, col0 : col0 + NB], in_=lm[:])
+
+        nc.gpsimd.memset(zeros[:], 0.0)
+        zero(xs_raw, 0, XS)
+        zero(wp[0], 0, WS)
+        zero(xs_raw, XS, G * XS)
+        zero(wp[0], WS, G * WS)
+
+        load_x_words(0, 1)
+        load_x_scales(0, 1)
+        load_w_words(0, 0, 0, 1)
+        load_w_scales(0, 0, 0, 1)
+        load_x_words(1, 4)
+        load_x_scales(1, G)
+        load_w_words(0, 0, 1, 2)
+        load_w_scales(0, 0, 1, 4)
+        load_w_words(0, 0, 2, 3)
+        load_w_words(0, 0, 3, 4)
+        load_x_words(4, G)
+        load_w_words(0, 0, 4, 5)
+        load_w_scales(0, 0, 4, G)
+        load_w_words(0, 0, 5, 6)
+        load_w_words(0, 0, 6, 7)
+        load_w_words(0, 0, 7, 8)
+
+        split_x(0, True)
+        split_x(1, False)
+        zero(wp[1], 0, G * WS // 2)
+        split_x(2, False)
+        zero(wp[1], G * WS // 2, G * WS)
+        for g in range(0, G, 2):
+            load_w_words(2, 1, g, g + 2)
+        load_w_scales(2, 1, 0, G)
+        split_x(3, False)
+        zero(wp[2], 0, G * WS // 2)
+        split_x(4, False)
+        zero(wp[2], G * WS // 2, G * WS)
+        for g in range(0, G, 2):
+            load_w_words(3, 2, g, g + 2)
+        load_w_scales(3, 2, 0, G)
+        for g in range(5, G):
+            split_x(g, False)
+
+        for i in range(WARM):
+            nc.tensor.matmul(out=banks[7][:], lhsT=zeros[:, 0:P], rhs=zeros[:], start=True, stop=True)
+
+        for g in range(G):
+            for c in range(QB):
+                for half in range(2):
+                    for par in range(2):
+                        mm(banks[2 * c + half], g, par, half, 0, c, g == 0 and par == 0, g == G - 1 and par == 1)
+        for c in range(QB):
+            for half in range(2):
+                keys_out(banks[2 * c + half], c * NB, half, half == 0, nc.gpsimd)
+
+        for g in range(0, G, 2):
+            load_w_words(1, 0, g, g + 2)
+        load_w_scales(1, 0, 0, G)
+
+        nxt = 0
+        for quad in (2, 3):
+            for c in range(QB):
+                for half in range(2):
+                    be = banks[nxt % 8]
+                    bo = banks[(nxt + 1) % 8]
+                    nxt += 2
+                    for g in range(G):
+                        mm(be, g, 0, half, quad - 1, c, g == 0, g == G - 1)
+                    for g in range(G):
+                        mm(bo, g, 1, half, quad - 1, c, g == 0, g == G - 1)
+                    values_out(be, bo, (quad - 2) * WS + c * NB, half)
+
+        for c in range(QB):
+            for half in range(2):
+                bk = banks[nxt % 8]
+                nxt += 1
+                for g in range(G):
+                    for par in range(2):
+                        mm(bk, g, par, half, 0, c, g == 0 and par == 0, g == G - 1 and par == 1)
+                last = c == QB - 1
+                keys_out(bk, WS + c * NB, half, half == 0, nc.sync if last else nc.gpsimd)

@@ -60,24 +60,29 @@ def tile_ammattention_pa_kernel(tc, x_words, x_scales, w_kv_words, w_kv_scales, 
             )
 
         def load_x_scales(g0, g1):
-            for q in range(4):
+            for r in range(4):
                 nc.sync.dma_start(
-                    out=xs_raw[32 * q : 32 * q + 4, g0 * XS : g1 * XS].rearrange("p (g n) -> p g n", g=g1 - g0).bitcast(I32),
-                    in_=x_scales[g0:g1, 4 * q : 4 * q + 4, :].rearrange("g r n -> r g n").bitcast(I32),
+                    out=xs_raw[r : P : 32, g0 * XS : g1 * XS].rearrange("p (g n) -> p g n", g=g1 - g0).bitcast(I32),
+                    in_=x_scales[g0:g1, r : 16 : 4, :].rearrange("g q n -> q g n").bitcast(I32),
                 )
 
-        def load_w_words(quad, slot, g0, g1):
+        def load_w_words(quad, slot, g0, g1, c0=0, c1=QB):
             nc.sync.dma_start(
-                out=ww[slot][:, g0 * WW : g1 * WW].rearrange("p (g n) -> p g n", g=g1 - g0).bitcast(I32),
-                in_=w_kv_words[g0:g1, :, quad * WW : (quad + 1) * WW].rearrange("g p n -> p g n").bitcast(I32),
+                out=ww[slot].rearrange("p (g n) -> p g n", g=G)[:, g0:g1, c0 * 2 * NB : c1 * 2 * NB].bitcast(I32),
+                in_=w_kv_words[g0:g1, :, quad * WW + c0 * 2 * NB : quad * WW + c1 * 2 * NB].rearrange("g p n -> p g n").bitcast(I32),
             )
 
-        def load_w_scales(quad, slot, g0, g1):
-            for q in range(4):
+        def load_w_scales(quad, slot, g0, g1, c0=0, c1=QB):
+            for r in range(4):
                 nc.sync.dma_start(
-                    out=wp[slot][32 * q : 32 * q + 4, g0 * WS : g1 * WS].rearrange("p (g n) -> p g n", g=g1 - g0).bitcast(I32),
-                    in_=w_kv_scales[g0:g1, 4 * q : 4 * q + 4, quad * WS : (quad + 1) * WS].rearrange("g r n -> r g n").bitcast(I32),
+                    out=wp[slot].rearrange("p (g n) -> p g n", g=G)[r : P : 32, g0:g1, c0 * NB : c1 * NB].bitcast(I32),
+                    in_=w_kv_scales[g0:g1, r : 16 : 4, quad * WS + c0 * NB : quad * WS + c1 * NB].rearrange("g q n -> q g n").bitcast(I32),
                 )
+
+        def load_quad(quad, slot):
+            for c0 in range(0, QB, 2):
+                load_w_scales(quad, slot, 0, G, c0, c0 + 2)
+                load_w_words(quad, slot, 0, G, c0, c0 + 2)
 
         def split_x(g, pieces):
             w_in = xw_raw[:, g * XW : (g + 1) * XW].rearrange("p (l par b) -> p par l b", par=2, b=2)
@@ -94,26 +99,26 @@ def tile_ammattention_pa_kernel(tc, x_words, x_scales, w_kv_words, w_kv_scales, 
                 nc.vector.tensor_copy(out=w_out, in_=w_in)
                 nc.vector.tensor_copy(out=s_out, in_=s_in)
 
-        def mm(bank, g, par, half, slot, c, start, stop):
+        def mm(bank, g, par, half, slot, c, start, stop, lo=0, n=NB):
             xo = g * XW + par * 512 + half * 256
             so = g * XS + par * 256 + half * 128
             nc.tensor.matmul_mx(
-                out=bank[:],
+                out=bank[:, 0:n],
                 lhsT=xw[:, xo : xo + 256].bitcast(FP4X4),
                 lhsT_scale=xs[:, so : so + 128],
-                rhs=ww[slot][:, g * WW + c * 2 * NB : g * WW + (c + 1) * 2 * NB].bitcast(FP4X4),
-                rhs_scale=wp[slot][:, g * WS + c * NB : g * WS + (c + 1) * NB],
+                rhs=ww[slot][:, g * WW + (c * NB + lo) * 2 : g * WW + (c * NB + lo + n) * 2].bitcast(FP4X4),
+                rhs_scale=wp[slot][:, g * WS + c * NB + lo : g * WS + c * NB + lo + n],
                 start=start,
                 stop=stop,
             )
 
-        def keys_out(bank, col0, half, on_scalar, queue):
+        def keys_out(bank, col0, half, on_scalar, queue, n=NB):
             kl = stage.tile([P, NB], F32, name="kl", tag="kl", bufs=4)
             if on_scalar:
-                nc.scalar.activation(out=kl[:], in_=bank[:], func=ACT.Copy, scale=0.5)
+                nc.scalar.activation(out=kl[:, 0:n], in_=bank[:, 0:n], func=ACT.Copy, scale=0.5)
             else:
-                nc.vector.tensor_scalar_mul(out=kl[:], in0=bank[:], scalar1=0.5)
-            queue.dma_start(out=out_1[0, half * P : (half + 1) * P, col0 : col0 + NB], in_=kl[:])
+                nc.vector.tensor_scalar_mul(out=kl[:, 0:n], in0=bank[:, 0:n], scalar1=0.5)
+            queue.dma_start(out=out_1[0, half * P : (half + 1) * P, col0 : col0 + n], in_=kl[:, 0:n])
 
         def values_out(bank_e, bank_o, col0, half):
             vt = stage.tile([P, 2, NB], F32, name="vt", tag="vt", bufs=3)
@@ -127,61 +132,61 @@ def tile_ammattention_pa_kernel(tc, x_words, x_scales, w_kv_words, w_kv_scales, 
             nc.gpsimd.dma_start(out=out_2[0, half * P : (half + 1) * P, col0 : col0 + NB], in_=lm[:])
 
         nc.gpsimd.memset(zeros[:], 0.0)
-        zero(xs_raw, 0, XS)
+        zero(xs_raw, 0, 2 * XS)
         zero(wp[0], 0, WS)
-        zero(xs_raw, XS, G * XS)
-        zero(wp[0], WS, G * WS)
+        zero(wp[0], WS, 4 * WS)
+        zero(xs_raw, 2 * XS, G * XS)
 
         load_x_words(0, 1)
-        load_x_scales(0, 1)
-        load_w_words(0, 0, 0, 1)
+        load_w_words(0, 0, 0, 1, 0, 2)
+        load_x_scales(0, 2)
         load_w_scales(0, 0, 0, 1)
+        load_w_words(0, 0, 0, 1, 2, 4)
         load_x_words(1, 4)
-        load_x_scales(1, G)
         load_w_words(0, 0, 1, 2)
         load_w_scales(0, 0, 1, 4)
+        load_x_scales(2, G)
         load_w_words(0, 0, 2, 3)
         load_w_words(0, 0, 3, 4)
         load_x_words(4, G)
-        load_w_words(0, 0, 4, 5)
-        load_w_scales(0, 0, 4, G)
-        load_w_words(0, 0, 5, 6)
-        load_w_words(0, 0, 6, 7)
-        load_w_words(0, 0, 7, 8)
 
         split_x(0, True)
+        zero(wp[0], 4 * WS, G * WS)
+        load_w_scales(0, 0, 4, G)
+        for g in range(4, G):
+            load_w_words(0, 0, g, g + 1)
+
         split_x(1, False)
         zero(wp[1], 0, G * WS // 2)
         split_x(2, False)
         zero(wp[1], G * WS // 2, G * WS)
-        for g in range(0, G, 2):
-            load_w_words(2, 1, g, g + 2)
-        load_w_scales(2, 1, 0, G)
+        load_quad(2, 1)
         split_x(3, False)
         zero(wp[2], 0, G * WS // 2)
         split_x(4, False)
         zero(wp[2], G * WS // 2, G * WS)
-        for g in range(0, G, 2):
-            load_w_words(3, 2, g, g + 2)
-        load_w_scales(3, 2, 0, G)
+        load_quad(3, 2)
         for g in range(5, G):
             split_x(g, False)
 
         for i in range(WARM):
             nc.tensor.matmul(out=banks[7][:], lhsT=zeros[:, 0:P], rhs=zeros[:], start=True, stop=True)
 
-        for g in range(G):
+        for c0 in range(0, QB, 2):
+            for half in range(2):
+                for par in range(2):
+                    for c in (c0, c0 + 1):
+                        mm(banks[2 * c + half], 0, par, half, 0, c, par == 0, False)
+        for g in range(1, G):
             for c in range(QB):
                 for half in range(2):
                     for par in range(2):
-                        mm(banks[2 * c + half], g, par, half, 0, c, g == 0 and par == 0, g == G - 1 and par == 1)
+                        mm(banks[2 * c + half], g, par, half, 0, c, False, g == G - 1 and par == 1)
         for c in range(QB):
             for half in range(2):
                 keys_out(banks[2 * c + half], c * NB, half, half == 0, nc.gpsimd)
 
-        for g in range(0, G, 2):
-            load_w_words(1, 0, g, g + 2)
-        load_w_scales(1, 0, 0, G)
+        load_quad(1, 0)
 
         nxt = 0
         for quad in (2, 3):
@@ -198,10 +203,18 @@ def tile_ammattention_pa_kernel(tc, x_words, x_scales, w_kv_words, w_kv_scales, 
 
         for c in range(QB):
             for half in range(2):
+                if c == QB - 1 and half == 1:
+                    continue
                 bk = banks[nxt % 8]
                 nxt += 1
                 for g in range(G):
                     for par in range(2):
                         mm(bk, g, par, half, 0, c, g == 0 and par == 0, g == G - 1 and par == 1)
-                last = c == QB - 1
-                keys_out(bk, WS + c * NB, half, half == 0, nc.sync if last else nc.gpsimd)
+                keys_out(bk, WS + c * NB, half, half == 0, nc.sync if c == QB - 1 else nc.gpsimd)
+        for part in range(2):
+            bk = banks[nxt % 8]
+            nxt += 1
+            for g in range(G):
+                for par in range(2):
+                    mm(bk, g, par, 1, 0, QB - 1, g == 0 and par == 0, g == G - 1 and par == 1, part * 256, 256)
+            keys_out(bk, WS + (QB - 1) * NB + part * 256, 1, part == 1, nc.scalar if part == 1 else nc.sync, 256)

@@ -21,6 +21,7 @@ XS = 512
 WW = QB * NB * 2
 WS = QB * NB
 WARM = 8
+QUADRANTS = (0, 2, 1, 3)
 
 
 def tile_ammattention_pa_kernel(tc, x_words, x_scales, w_kv_words, w_kv_scales, out_0, out_1, out_2):
@@ -60,10 +61,10 @@ def tile_ammattention_pa_kernel(tc, x_words, x_scales, w_kv_words, w_kv_scales, 
             )
 
         def load_x_scales(g0, g1):
-            for r in range(4):
+            for q in QUADRANTS:
                 nc.sync.dma_start(
-                    out=xs_raw[r : P : 32, g0 * XS : g1 * XS].rearrange("p (g n) -> p g n", g=g1 - g0).bitcast(I32),
-                    in_=x_scales[g0:g1, r : 16 : 4, :].rearrange("g q n -> q g n").bitcast(I32),
+                    out=xs_raw[32 * q : 32 * q + 4, g0 * XS : g1 * XS].rearrange("p (g n) -> p g n", g=g1 - g0).bitcast(I32),
+                    in_=x_scales[g0:g1, 4 * q : 4 * q + 4, :].rearrange("g r n -> r g n").bitcast(I32),
                 )
 
         def load_w_words(quad, slot, g0, g1, c0=0, c1=QB):
@@ -73,10 +74,10 @@ def tile_ammattention_pa_kernel(tc, x_words, x_scales, w_kv_words, w_kv_scales, 
             )
 
         def load_w_scales(quad, slot, g0, g1, c0=0, c1=QB):
-            for r in range(4):
+            for q in QUADRANTS:
                 nc.sync.dma_start(
-                    out=wp[slot].rearrange("p (g n) -> p g n", g=G)[r : P : 32, g0:g1, c0 * NB : c1 * NB].bitcast(I32),
-                    in_=w_kv_scales[g0:g1, r : 16 : 4, quad * WS + c0 * NB : quad * WS + c1 * NB].rearrange("g q n -> q g n").bitcast(I32),
+                    out=wp[slot].rearrange("p (g n) -> p g n", g=G)[32 * q : 32 * q + 4, g0:g1, c0 * NB : c1 * NB].bitcast(I32),
+                    in_=w_kv_scales[g0:g1, 4 * q : 4 * q + 4, quad * WS + c0 * NB : quad * WS + c1 * NB].rearrange("g r n -> r g n").bitcast(I32),
                 )
 
         def load_quad(quad, slot):
@@ -142,9 +143,9 @@ def tile_ammattention_pa_kernel(tc, x_words, x_scales, w_kv_words, w_kv_scales, 
         load_x_scales(0, 2)
         load_w_scales(0, 0, 0, 1)
         load_w_words(0, 0, 0, 1, 2, 4)
+        load_w_scales(0, 0, 1, 4)
         load_x_words(1, 4)
         load_w_words(0, 0, 1, 2)
-        load_w_scales(0, 0, 1, 4)
         load_x_scales(2, G)
         load_w_words(0, 0, 2, 3)
         load_w_words(0, 0, 3, 4)

@@ -92,10 +92,9 @@ def tile_ammattention_pa_kernel(tc, x_words, x_scales, w_kv_words, w_kv_scales, 
             s_out = xs[:, g * XS : (g + 1) * XS].rearrange("p (par l) -> p par l", par=2)
             if pieces:
                 for half in range(2):
-                    for par in range(2):
-                        rows = slice(half * P, (half + 1) * P)
-                        nc.vector.tensor_copy(out=w_out[:, par, rows, :], in_=w_in[:, par, rows, :])
-                        nc.vector.tensor_copy(out=s_out[:, par, rows], in_=s_in[:, par, rows])
+                    rows = slice(half * P, (half + 1) * P)
+                    nc.vector.tensor_copy(out=w_out[:, :, rows, :], in_=w_in[:, :, rows, :])
+                    nc.vector.tensor_copy(out=s_out[:, :, rows], in_=s_in[:, :, rows])
             else:
                 nc.vector.tensor_copy(out=w_out, in_=w_in)
                 nc.vector.tensor_copy(out=s_out, in_=s_in)
@@ -126,9 +125,9 @@ def tile_ammattention_pa_kernel(tc, x_words, x_scales, w_kv_words, w_kv_scales, 
             he = stage.tile([P, NB], F32, name="he", tag="he", bufs=2)
             lm = stage.tile([P, NB], F32, name="lm", tag="lm", bufs=3)
             nc.scalar.copy(out=vt[:, 0, :], in_=bank_e[:])
-            nc.scalar.activation(out=he[:], in_=bank_e[:], func=ACT.Copy, scale=0.5)
+            nc.scalar.activation(out=he[:], in_=vt[:, 0, :], func=ACT.Copy, scale=0.5)
             nc.vector.tensor_copy(out=vt[:, 1, :], in_=bank_o[:])
-            nc.vector.scalar_tensor_tensor(out=lm[:], in0=bank_o[:], scalar=0.5, in1=he[:], op0=ALU.mult, op1=ALU.add)
+            nc.vector.scalar_tensor_tensor(out=lm[:], in0=vt[:, 1, :], scalar=0.5, in1=he[:], op0=ALU.mult, op1=ALU.add)
             nc.gpsimd.dma_start(out=v_view[half, :, :, col0 : col0 + NB], in_=vt[:])
             nc.gpsimd.dma_start(out=out_2[0, half * P : (half + 1) * P, col0 : col0 + NB], in_=lm[:])
 
@@ -143,8 +142,8 @@ def tile_ammattention_pa_kernel(tc, x_words, x_scales, w_kv_words, w_kv_scales, 
         load_x_scales(0, 2)
         load_w_scales(0, 0, 0, 1)
         load_w_words(0, 0, 0, 1, 2, 4)
-        load_w_scales(0, 0, 1, 4)
         load_x_words(1, 4)
+        load_w_scales(0, 0, 1, 4)
         load_w_words(0, 0, 1, 2)
         load_x_scales(2, G)
         load_w_words(0, 0, 2, 3)
@@ -152,12 +151,12 @@ def tile_ammattention_pa_kernel(tc, x_words, x_scales, w_kv_words, w_kv_scales, 
         load_x_words(4, G)
 
         split_x(0, True)
+        split_x(1, False)
         zero(wp[0], 4 * WS, G * WS)
         load_w_scales(0, 0, 4, G)
         for g in range(4, G):
             load_w_words(0, 0, g, g + 1)
 
-        split_x(1, False)
         zero(wp[1], 0, G * WS // 2)
         split_x(2, False)
         zero(wp[1], G * WS // 2, G * WS)

@@ -92,9 +92,10 @@ def tile_ammattention_pa_kernel(tc, x_words, x_scales, w_kv_words, w_kv_scales, 
             s_out = xs[:, g * XS : (g + 1) * XS].rearrange("p (par l) -> p par l", par=2)
             if pieces:
                 for half in range(2):
-                    rows = slice(half * P, (half + 1) * P)
-                    nc.vector.tensor_copy(out=w_out[:, :, rows, :], in_=w_in[:, :, rows, :])
-                    nc.vector.tensor_copy(out=s_out[:, :, rows], in_=s_in[:, :, rows])
+                    for par in range(2):
+                        rows = slice(half * P, (half + 1) * P)
+                        nc.vector.tensor_copy(out=w_out[:, par, rows, :], in_=w_in[:, par, rows, :])
+                        nc.vector.tensor_copy(out=s_out[:, par, rows], in_=s_in[:, par, rows])
             else:
                 nc.vector.tensor_copy(out=w_out, in_=w_in)
                 nc.vector.tensor_copy(out=s_out, in_=s_in)
@@ -125,9 +126,9 @@ def tile_ammattention_pa_kernel(tc, x_words, x_scales, w_kv_words, w_kv_scales, 
             he = stage.tile([P, NB], F32, name="he", tag="he", bufs=2)
             lm = stage.tile([P, NB], F32, name="lm", tag="lm", bufs=3)
             nc.scalar.copy(out=vt[:, 0, :], in_=bank_e[:])
-            nc.scalar.activation(out=he[:], in_=vt[:, 0, :], func=ACT.Copy, scale=0.5)
+            nc.scalar.activation(out=he[:], in_=bank_e[:], func=ACT.Copy, scale=0.5)
             nc.vector.tensor_copy(out=vt[:, 1, :], in_=bank_o[:])
-            nc.vector.scalar_tensor_tensor(out=lm[:], in0=vt[:, 1, :], scalar=0.5, in1=he[:], op0=ALU.mult, op1=ALU.add)
+            nc.vector.scalar_tensor_tensor(out=lm[:], in0=bank_o[:], scalar=0.5, in1=he[:], op0=ALU.mult, op1=ALU.add)
             nc.gpsimd.dma_start(out=v_view[half, :, :, col0 : col0 + NB], in_=vt[:])
             nc.gpsimd.dma_start(out=out_2[0, half * P : (half + 1) * P, col0 : col0 + NB], in_=lm[:])
 
@@ -142,32 +143,40 @@ def tile_ammattention_pa_kernel(tc, x_words, x_scales, w_kv_words, w_kv_scales, 
         load_x_scales(0, 2)
         load_w_scales(0, 0, 0, 1)
         load_w_words(0, 0, 0, 1, 2, 4)
-        load_x_words(1, 4)
-        load_w_scales(0, 0, 1, 4)
+        load_x_words(1, 2)
+        load_w_scales(0, 0, 1, 2)
         load_w_words(0, 0, 1, 2)
-        load_x_scales(2, G)
+        load_x_words(2, 4)
         load_w_words(0, 0, 2, 3)
+        load_x_scales(2, 4)
+        load_w_scales(0, 0, 2, 3)
+        load_w_scales(0, 0, 3, 4)
         load_w_words(0, 0, 3, 4)
         load_x_words(4, G)
+        load_x_scales(4, G)
 
         split_x(0, True)
         split_x(1, False)
         zero(wp[0], 4 * WS, G * WS)
-        load_w_scales(0, 0, 4, G)
-        for g in range(4, G):
-            load_w_words(0, 0, g, g + 1)
+        load_w_scales(0, 0, 4, 6)
+        load_w_words(0, 0, 4, 5)
+        load_w_words(0, 0, 5, 6)
+        load_w_scales(0, 0, 6, G)
+        load_w_words(0, 0, 6, 7)
+        load_w_words(0, 0, 7, G)
 
-        zero(wp[1], 0, G * WS // 2)
         split_x(2, False)
+        zero(wp[1], 0, G * WS // 2)
+        split_x(3, False)
         zero(wp[1], G * WS // 2, G * WS)
         load_quad(2, 1)
-        split_x(3, False)
-        zero(wp[2], 0, G * WS // 2)
         split_x(4, False)
+        zero(wp[2], 0, G * WS // 2)
+        split_x(5, False)
         zero(wp[2], G * WS // 2, G * WS)
         load_quad(3, 2)
-        for g in range(5, G):
-            split_x(g, False)
+        split_x(6, False)
+        split_x(7, False)
 
         for i in range(WARM):
             nc.tensor.matmul(out=banks[7][:], lhsT=zeros[:, 0:P], rhs=zeros[:], start=True, stop=True)

@@ -20,6 +20,7 @@ XW = 1024
 XS = 512
 WW = QB * NB * 2
 WS = QB * NB
+XP = 12
 WARM = 8
 QUADRANTS = (0, 2, 1, 3)
 
@@ -32,13 +33,13 @@ def tile_ammattention_pa_kernel(tc, x_words, x_scales, w_kv_words, w_kv_scales, 
         psum = ctx.enter_context(tc.psum_pool(name="psum", bufs=1))
         ctx.enter_context(tc.manual_schedule())
 
-        xw_raw = keep.tile([P, G * XW], U8, name="xw_raw", align_bytes=256)
-        xs_raw = keep.tile([P, G * XS], U8, name="xs_raw", align_bytes=256)
-        xw = keep.tile([P, G * XW], U8, name="xw", align_bytes=256)
-        xs = keep.tile([P, G * XS], U8, name="xs", align_bytes=256)
+        xw_raw = keep.tile([P, XP * XW], U8, name="xw_raw", align_bytes=256)
+        xs_raw = keep.tile([P, XP * XS], U8, name="xs_raw", align_bytes=256)
+        xw = keep.tile([P, XP * XW], U8, name="xw", align_bytes=256)
+        xs = keep.tile([P, XP * XS], U8, name="xs", align_bytes=256)
         ww = []
         wp = []
-        for s in range(3):
+        for s in range(2):
             ww_s = keep.tile([P, G * WW], U8, name="ww%d" % s, align_bytes=256)
             wp_s = keep.tile([P, G * WS], U8, name="wp%d" % s, align_bytes=256)
             ww.append(ww_s)
@@ -114,7 +115,7 @@ def tile_ammattention_pa_kernel(tc, x_words, x_scales, w_kv_words, w_kv_scales, 
             )
 
         def keys_out(bank, col0, half, on_scalar, queue, n=NB):
-            kl = stage.tile([P, NB], F32, name="kl", tag="kl", bufs=4)
+            kl = stage.tile([P, NB], F32, name="kl", tag="kl", bufs=8)
             if on_scalar:
                 nc.scalar.activation(out=kl[:, 0:n], in_=bank[:, 0:n], func=ACT.Copy, scale=0.5)
             else:
@@ -122,9 +123,9 @@ def tile_ammattention_pa_kernel(tc, x_words, x_scales, w_kv_words, w_kv_scales, 
             queue.dma_start(out=out_1[0, half * P : (half + 1) * P, col0 : col0 + n], in_=kl[:, 0:n])
 
         def values_out(bank_e, bank_o, col0, half):
-            vt = stage.tile([P, 2, NB], F32, name="vt", tag="vt", bufs=3)
-            he = stage.tile([P, NB], F32, name="he", tag="he", bufs=2)
-            lm = stage.tile([P, NB], F32, name="lm", tag="lm", bufs=3)
+            vt = stage.tile([P, 2, NB], F32, name="vt", tag="vt", bufs=6)
+            he = stage.tile([P, NB], F32, name="he", tag="he", bufs=3)
+            lm = stage.tile([P, NB], F32, name="lm", tag="lm", bufs=6)
             nc.scalar.copy(out=vt[:, 0, :], in_=bank_e[:])
             nc.scalar.activation(out=he[:], in_=bank_e[:], func=ACT.Copy, scale=0.5)
             nc.vector.tensor_copy(out=vt[:, 1, :], in_=bank_o[:])
@@ -171,10 +172,7 @@ def tile_ammattention_pa_kernel(tc, x_words, x_scales, w_kv_words, w_kv_scales, 
         zero(wp[1], G * WS // 2, G * WS)
         load_quad(2, 1)
         split_x(4, False)
-        zero(wp[2], 0, G * WS // 2)
         split_x(5, False)
-        zero(wp[2], G * WS // 2, G * WS)
-        load_quad(3, 2)
         split_x(6, False)
         split_x(7, False)
 
@@ -187,28 +185,30 @@ def tile_ammattention_pa_kernel(tc, x_words, x_scales, w_kv_words, w_kv_scales, 
                     for c in (c0, c0 + 1):
                         mm(banks[2 * c + half], 0, par, half, 0, c, par == 0, False)
         for g in range(1, G):
-            for c in range(QB):
-                for half in range(2):
-                    for par in range(2):
+            for half in range(2):
+                for par in range(2):
+                    for c in range(QB):
                         mm(banks[2 * c + half], g, par, half, 0, c, False, g == G - 1 and par == 1)
         for c in range(QB):
             for half in range(2):
                 keys_out(banks[2 * c + half], c * NB, half, half == 0, nc.gpsimd)
 
-        load_quad(1, 0)
+        load_quad(3, 0)
 
         nxt = 0
-        for quad in (2, 3):
+        for quad, slot in ((2, 1), (3, 0)):
             for c in range(QB):
                 for half in range(2):
                     be = banks[nxt % 8]
                     bo = banks[(nxt + 1) % 8]
                     nxt += 2
                     for g in range(G):
-                        mm(be, g, 0, half, quad - 1, c, g == 0, g == G - 1)
+                        mm(be, g, 0, half, slot, c, g == 0, g == G - 1)
                     for g in range(G):
-                        mm(bo, g, 1, half, quad - 1, c, g == 0, g == G - 1)
+                        mm(bo, g, 1, half, slot, c, g == 0, g == G - 1)
                     values_out(be, bo, (quad - 2) * WS + c * NB, half)
+            if quad == 2:
+                load_quad(1, 1)
 
         for c in range(QB):
             for half in range(2):
@@ -218,12 +218,12 @@ def tile_ammattention_pa_kernel(tc, x_words, x_scales, w_kv_words, w_kv_scales, 
                 nxt += 1
                 for g in range(G):
                     for par in range(2):
-                        mm(bk, g, par, half, 0, c, g == 0 and par == 0, g == G - 1 and par == 1)
+                        mm(bk, g, par, half, 1, c, g == 0 and par == 0, g == G - 1 and par == 1)
                 keys_out(bk, WS + c * NB, half, half == 0, nc.sync if c == QB - 1 else nc.gpsimd)
         for part in range(2):
             bk = banks[nxt % 8]
             nxt += 1
             for g in range(G):
                 for par in range(2):
-                    mm(bk, g, par, 1, 0, QB - 1, g == 0 and par == 0, g == G - 1 and par == 1, part * 256, 256)
+                    mm(bk, g, par, 1, 1, QB - 1, g == 0 and par == 0, g == G - 1 and par == 1, part * 256, 256)
             keys_out(bk, WS + (QB - 1) * NB + part * 256, 1, part == 1, nc.scalar if part == 1 else nc.sync, 256)

@@ -21,7 +21,7 @@ XS = 512
 WW = QB * NB * 2
 WS = QB * NB
 XP = 12
-WARM = 8
+WARM = 5
 QUADRANTS = (0, 2, 1, 3)
 
 

@@ -21,7 +21,7 @@ XS = 512
 WW = QB * NB * 2
 WS = QB * NB
 XP = 12
-WARM = 5
+WARM = 6
 QUADRANTS = (0, 2, 1, 3)
 
 
@@ -59,6 +59,12 @@ def tile_ammattention_pa_kernel(tc, x_words, x_scales, w_kv_words, w_kv_scales, 
             nc.sync.dma_start(
                 out=xw_raw[:, g0 * XW : g1 * XW].rearrange("p (g n) -> p g n", g=g1 - g0).bitcast(I32),
                 in_=x_words[g0:g1].rearrange("g p n -> p g n").bitcast(I32),
+            )
+
+        def load_x_words_half(g, half):
+            nc.sync.dma_start(
+                out=xw_raw[:, g * XW + half * 512 : g * XW + (half + 1) * 512].bitcast(I32),
+                in_=x_words[g, :, half * 512 : (half + 1) * 512].bitcast(I32),
             )
 
         def load_x_scales(g0, g1):
@@ -133,16 +139,18 @@ def tile_ammattention_pa_kernel(tc, x_words, x_scales, w_kv_words, w_kv_scales, 
             nc.gpsimd.dma_start(out=v_view[half, :, :, col0 : col0 + NB], in_=vt[:])
             nc.gpsimd.dma_start(out=out_2[0, half * P : (half + 1) * P, col0 : col0 + NB], in_=lm[:])
 
-        nc.gpsimd.memset(zeros[:], 0.0)
-        zero(xs_raw, 0, 2 * XS)
-        zero(wp[0], 0, WS)
+        nc.gpsimd.memset(xs_raw[:, 0 : 2 * XS].bitcast(F32), 0.0)
+        nc.gpsimd.memset(wp[0][:, 0:WS].bitcast(F32), 0.0)
+        nc.vector.memset(zeros[:], 0.0)
         zero(wp[0], WS, 4 * WS)
         zero(xs_raw, 2 * XS, G * XS)
 
-        load_x_words(0, 1)
-        load_w_words(0, 0, 0, 1, 0, 2)
+        load_x_words_half(0, 0)
         load_x_scales(0, 2)
+        load_w_words(0, 0, 0, 1, 0, 1)
         load_w_scales(0, 0, 0, 1)
+        load_w_words(0, 0, 0, 1, 1, 2)
+        load_x_words_half(0, 1)
         load_w_words(0, 0, 0, 1, 2, 4)
         load_x_words(1, 2)
         load_w_scales(0, 0, 1, 2)

@@ -133,9 +133,9 @@ def tile_ammattention_pa_kernel(tc, x_words, x_scales, w_kv_words, w_kv_scales, 
             he = stage.tile([P, NB], F32, name="he", tag="he", bufs=3)
             lm = stage.tile([P, NB], F32, name="lm", tag="lm", bufs=6)
             nc.scalar.copy(out=vt[:, 0, :], in_=bank_e[:])
-            nc.scalar.activation(out=he[:], in_=bank_e[:], func=ACT.Copy, scale=0.5)
-            nc.vector.tensor_copy(out=vt[:, 1, :], in_=bank_o[:])
-            nc.vector.scalar_tensor_tensor(out=lm[:], in0=bank_o[:], scalar=0.5, in1=he[:], op0=ALU.mult, op1=ALU.add)
+            nc.scalar.copy(out=vt[:, 1, :], in_=bank_o[:])
+            nc.vector.tensor_tensor(out=he[:], in0=vt[:, 0, :], in1=vt[:, 1, :], op=ALU.add)
+            nc.vector.tensor_scalar_mul(out=lm[:], in0=he[:], scalar1=0.5)
             nc.gpsimd.dma_start(out=v_view[half, :, :, col0 : col0 + NB], in_=vt[:])
             nc.gpsimd.dma_start(out=out_2[0, half * P : (half + 1) * P, col0 : col0 + NB], in_=lm[:])
 
@@ -199,7 +199,7 @@ def tile_ammattention_pa_kernel(tc, x_words, x_scales, w_kv_words, w_kv_scales, 
                         mm(banks[2 * c + half], g, par, half, 0, c, False, g == G - 1 and par == 1)
         for c in range(QB):
             for half in range(2):
-                keys_out(banks[2 * c + half], c * NB, half, half == 0, nc.gpsimd)
+                keys_out(banks[2 * c + half], c * NB, half, True, nc.gpsimd)
 
         load_quad(3, 0)
 
@@ -227,7 +227,7 @@ def tile_ammattention_pa_kernel(tc, x_words, x_scales, w_kv_words, w_kv_scales, 
                 for g in range(G):
                     for par in range(2):
                         mm(bk, g, par, half, 1, c, g == 0 and par == 0, g == G - 1 and par == 1)
-                keys_out(bk, WS + c * NB, half, half == 0, nc.sync if c == QB - 1 else nc.gpsimd)
+                keys_out(bk, WS + c * NB, half, True, nc.sync if c == QB - 1 else nc.gpsimd)
         for part in range(2):
             bk = banks[nxt % 8]
             nxt += 1

@@ -136,8 +136,8 @@ def tile_ammattention_pa_kernel(tc, x_words, x_scales, w_kv_words, w_kv_scales, 
             nc.scalar.copy(out=vt[:, 1, :], in_=bank_o[:])
             nc.vector.tensor_tensor(out=he[:], in0=vt[:, 0, :], in1=vt[:, 1, :], op=ALU.add)
             nc.vector.tensor_scalar_mul(out=lm[:], in0=he[:], scalar1=0.5)
-            nc.gpsimd.dma_start(out=v_view[half, :, :, col0 : col0 + NB], in_=vt[:])
-            nc.gpsimd.dma_start(out=out_2[0, half * P : (half + 1) * P, col0 : col0 + NB], in_=lm[:])
+            nc.sync.dma_start(out=v_view[half, :, :, col0 : col0 + NB], in_=vt[:])
+            nc.sync.dma_start(out=out_2[0, half * P : (half + 1) * P, col0 : col0 + NB], in_=lm[:])
 
         nc.gpsimd.memset(xs_raw[:, 0 : 2 * XS].bitcast(F32), 0.0)
         nc.gpsimd.memset(wp[0][:, 0:WS].bitcast(F32), 0.0)
@@ -199,7 +199,7 @@ def tile_ammattention_pa_kernel(tc, x_words, x_scales, w_kv_words, w_kv_scales, 
                         mm(banks[2 * c + half], g, par, half, 0, c, False, g == G - 1 and par == 1)
         for c in range(QB):
             for half in range(2):
-                keys_out(banks[2 * c + half], c * NB, half, True, nc.gpsimd)
+                keys_out(banks[2 * c + half], c * NB, half, True, nc.sync)
 
         load_quad(3, 0)
 
@@ -227,7 +227,7 @@ def tile_ammattention_pa_kernel(tc, x_words, x_scales, w_kv_words, w_kv_scales, 
                 for g in range(G):
                     for par in range(2):
                         mm(bk, g, par, half, 1, c, g == 0 and par == 0, g == G - 1 and par == 1)
-                keys_out(bk, WS + c * NB, half, True, nc.sync if c == QB - 1 else nc.gpsimd)
+                keys_out(bk, WS + c * NB, half, True, nc.sync)
         for part in range(2):
             bk = banks[nxt % 8]
             nxt += 1

@@ -139,8 +139,8 @@ def tile_ammattention_pa_kernel(tc, x_words, x_scales, w_kv_words, w_kv_scales, 
             nc.sync.dma_start(out=v_view[half, :, :, col0 : col0 + NB], in_=vt[:])
             nc.sync.dma_start(out=out_2[0, half * P : (half + 1) * P, col0 : col0 + NB], in_=lm[:])
 
-        nc.gpsimd.memset(xs_raw[:, 0 : 2 * XS].bitcast(F32), 0.0)
-        nc.gpsimd.memset(wp[0][:, 0:WS].bitcast(F32), 0.0)
+        zero(xs_raw, 0, 2 * XS)
+        zero(wp[0], 0, WS)
         nc.vector.memset(zeros[:], 0.0)
         zero(wp[0], WS, 4 * WS)
         zero(xs_raw, 2 * XS, G * XS)

@@ -234,4 +234,4 @@ def tile_ammattention_pa_kernel(tc, x_words, x_scales, w_kv_words, w_kv_scales, 
             for g in range(G):
                 for par in range(2):
                     mm(bk, g, par, 1, 1, QB - 1, g == 0 and par == 0, g == G - 1 and par == 1, part * 256, 256)
-            keys_out(bk, WS + (QB - 1) * NB + part * 256, 1, part == 1, nc.scalar if part == 1 else nc.sync, 256)
+            keys_out(bk, WS + (QB - 1) * NB + part * 256, 1, True, nc.sync, 256)

@@ -20,7 +20,6 @@ XW = 1024
 XS = 512
 WW = QB * NB * 2
 WS = QB * NB
-XP = 12
 WARM = 6
 QUADRANTS = (0, 2, 1, 3)
 
@@ -33,10 +32,10 @@ def tile_ammattention_pa_kernel(tc, x_words, x_scales, w_kv_words, w_kv_scales, 
         psum = ctx.enter_context(tc.psum_pool(name="psum", bufs=1))
         ctx.enter_context(tc.manual_schedule())
 
-        xw_raw = keep.tile([P, XP * XW], U8, name="xw_raw", align_bytes=256)
-        xs_raw = keep.tile([P, XP * XS], U8, name="xs_raw", align_bytes=256)
-        xw = keep.tile([P, XP * XW], U8, name="xw", align_bytes=256)
-        xs = keep.tile([P, XP * XS], U8, name="xs", align_bytes=256)
+        xw_raw = keep.tile([P, G * XW], U8, name="xw_raw", align_bytes=256)
+        xs_raw = keep.tile([P, G * XS], U8, name="xs_raw", align_bytes=256)
+        xw = keep.tile([P, G * XW], U8, name="xw", align_bytes=256)
+        xs = keep.tile([P, G * XS], U8, name="xs", align_bytes=256)
         ww = []
         wp = []
         for s in range(2):

@@ -188,8 +188,8 @@ def tile_ammattention_pa_kernel(tc, x_words, x_scales, w_kv_words, w_kv_scales, 
 
         for c0 in range(0, QB, 2):
             for half in range(2):
-                for par in range(2):
-                    for c in (c0, c0 + 1):
+                for c in (c0, c0 + 1):
+                    for par in range(2):
                         mm(banks[2 * c + half], 0, par, half, 0, c, par == 0, False)
         for g in range(1, G):
             for half in range(2):

from contextlib import ExitStack

import concourse.mybir as mybir

FLOPS = 2 * 512 * 4096 * 8192

F32 = mybir.dt.float32
BF16 = mybir.dt.bfloat16
I32 = mybir.dt.int32
U8 = mybir.dt.uint8
FP4X4 = mybir.dt.float4_e2m1fn_x4
ACT = mybir.ActivationFunctionType
ALU = mybir.AluOpType

P = 128
G = 8
NB = 512
QB = 4
XW = 1024
XS = 512
WW = QB * NB * 2
WS = QB * NB
WARM = 6
QUADRANTS = (0, 2, 1, 3)


def tile_ammattention_pa_kernel(tc, x_words, x_scales, w_kv_words, w_kv_scales, out_0, out_1, out_2):
    nc = tc.nc
    with ExitStack() as ctx:
        keep = ctx.enter_context(tc.tile_pool(name="keep", bufs=1))
        stage = ctx.enter_context(tc.tile_pool(name="stage", bufs=3))
        psum = ctx.enter_context(tc.psum_pool(name="psum", bufs=1))
        ctx.enter_context(tc.manual_schedule())

        xw_raw = keep.tile([P, G * XW], U8, name="xw_raw", align_bytes=256)
        xs_raw = keep.tile([P, G * XS], U8, name="xs_raw", align_bytes=256)
        xw = keep.tile([P, G * XW], U8, name="xw", align_bytes=256)
        xs = keep.tile([P, G * XS], U8, name="xs", align_bytes=256)
        ww = []
        wp = []
        for s in range(2):
            ww_s = keep.tile([P, G * WW], U8, name="ww%d" % s, align_bytes=256)
            wp_s = keep.tile([P, G * WS], U8, name="wp%d" % s, align_bytes=256)
            ww.append(ww_s)
            wp.append(wp_s)
        zeros = keep.tile([P, NB], BF16, name="zeros", align_bytes=256)
        banks = []
        for b in range(8):
            bank_b = psum.tile([P, NB], F32, name="bank%d" % b)
            banks.append(bank_b)

        v_view = out_0.rearrange("b (j l two) c -> (b j) l two c", l=P, two=2)

        def zero(t, lo, hi):
            nc.vector.memset(t[:, lo:hi].bitcast(I32), 0)

        def load_x_words(g0, g1):
            nc.sync.dma_start(
                out=xw_raw[:, g0 * XW : g1 * XW].rearrange("p (g n) -> p g n", g=g1 - g0).bitcast(I32),
                in_=x_words[g0:g1].rearrange("g p n -> p g n").bitcast(I32),
            )

        def load_x_words_half(g, half):
            nc.sync.dma_start(
                out=xw_raw[:, g * XW + half * 512 : g * XW + (half + 1) * 512].bitcast(I32),
                in_=x_words[g, :, half * 512 : (half + 1) * 512].bitcast(I32),
            )

        def load_x_scales(g0, g1):
            for q in QUADRANTS:
                nc.sync.dma_start(
                    out=xs_raw[32 * q : 32 * q + 4, g0 * XS : g1 * XS].rearrange("p (g n) -> p g n", g=g1 - g0).bitcast(I32),
                    in_=x_scales[g0:g1, 4 * q : 4 * q + 4, :].rearrange("g r n -> r g n").bitcast(I32),
                )

        def load_w_words(quad, slot, g0, g1, c0=0, c1=QB):
            nc.sync.dma_start(
                out=ww[slot].rearrange("p (g n) -> p g n", g=G)[:, g0:g1, c0 * 2 * NB : c1 * 2 * NB].bitcast(I32),
                in_=w_kv_words[g0:g1, :, quad * WW + c0 * 2 * NB : quad * WW + c1 * 2 * NB].rearrange("g p n -> p g n").bitcast(I32),
            )

        def load_w_scales(quad, slot, g0, g1, c0=0, c1=QB):
            for q in QUADRANTS:
                nc.sync.dma_start(
                    out=wp[slot].rearrange("p (g n) -> p g n", g=G)[32 * q : 32 * q + 4, g0:g1, c0 * NB : c1 * NB].bitcast(I32),
                    in_=w_kv_scales[g0:g1, 4 * q : 4 * q + 4, quad * WS + c0 * NB : quad * WS + c1 * NB].rearrange("g r n -> r g n").bitcast(I32),
                )

        def load_quad(quad, slot):
            for c0 in range(0, QB, 2):
                load_w_scales(quad, slot, 0, G, c0, c0 + 2)
                load_w_words(quad, slot, 0, G, c0, c0 + 2)

        def split_x(g, pieces):
            w_in = xw_raw[:, g * XW : (g + 1) * XW].rearrange("p (l par b) -> p par l b", par=2, b=2)
            w_out = xw[:, g * XW : (g + 1) * XW].rearrange("p (par l b) -> p par l b", par=2, b=2)
            s_in = xs_raw[:, g * XS : (g + 1) * XS].rearrange("p (l par) -> p par l", par=2)
            s_out = xs[:, g * XS : (g + 1) * XS].rearrange("p (par l) -> p par l", par=2)
            if pieces:
                for half in range(2):
                    for par in range(2):
                        rows = slice(half * P, (half + 1) * P)
                        nc.vector.tensor_copy(out=w_out[:, par, rows, :], in_=w_in[:, par, rows, :])
                        nc.vector.tensor_copy(out=s_out[:, par, rows], in_=s_in[:, par, rows])
            else:
                nc.vector.tensor_copy(out=w_out, in_=w_in)
                nc.vector.tensor_copy(out=s_out, in_=s_in)

        def mm(bank, g, par, half, slot, c, start, stop, lo=0, n=NB):
            xo = g * XW + par * 512 + half * 256
            so = g * XS + par * 256 + half * 128
            nc.tensor.matmul_mx(
                out=bank[:, 0:n],
                lhsT=xw[:, xo : xo + 256].bitcast(FP4X4),
                lhsT_scale=xs[:, so : so + 128],
                rhs=ww[slot][:, g * WW + (c * NB + lo) * 2 : g * WW + (c * NB + lo + n) * 2].bitcast(FP4X4),
                rhs_scale=wp[slot][:, g * WS + c * NB + lo : g * WS + c * NB + lo + n],
                start=start,
                stop=stop,
            )

        def keys_out(bank, col0, half, on_scalar, queue, n=NB):
            kl = stage.tile([P, NB], F32, name="kl", tag="kl", bufs=8)
            if on_scalar:
                nc.scalar.activation(out=kl[:, 0:n], in_=bank[:, 0:n], func=ACT.Copy, scale=0.5)
            else:
                nc.vector.tensor_scalar_mul(out=kl[:, 0:n], in0=bank[:, 0:n], scalar1=0.5)
            queue.dma_start(out=out_1[0, half * P : (half + 1) * P, col0 : col0 + n], in_=kl[:, 0:n])

        def values_out(bank_e, bank_o, col0, half):
            vt = stage.tile([P, 2, NB], F32, name="vt", tag="vt", bufs=6)
            he = stage.tile([P, NB], F32, name="he", tag="he", bufs=3)
            lm = stage.tile([P, NB], F32, name="lm", tag="lm", bufs=6)
            nc.scalar.copy(out=vt[:, 0, :], in_=bank_e[:])
            nc.scalar.copy(out=vt[:, 1, :], in_=bank_o[:])
            nc.vector.tensor_tensor(out=he[:], in0=vt[:, 0, :], in1=vt[:, 1, :], op=ALU.add)
            nc.vector.tensor_scalar_mul(out=lm[:], in0=he[:], scalar1=0.5)
            nc.sync.dma_start(out=v_view[half, :, :, col0 : col0 + NB], in_=vt[:])
            nc.sync.dma_start(out=out_2[0, half * P : (half + 1) * P, col0 : col0 + NB], in_=lm[:])

        zero(xs_raw, 0, 2 * XS)
        zero(wp[0], 0, WS)
        nc.vector.memset(zeros[:], 0.0)
        zero(wp[0], WS, 4 * WS)
        zero(xs_raw, 2 * XS, G * XS)

        load_x_words_half(0, 0)
        load_x_scales(0, 2)
        load_w_words(0, 0, 0, 1, 0, 1)
        load_w_scales(0, 0, 0, 1)
        load_w_words(0, 0, 0, 1, 1, 2)
        load_x_words_half(0, 1)
        load_w_words(0, 0, 0, 1, 2, 4)
        load_x_words(1, 2)
        load_w_scales(0, 0, 1, 2)
        load_w_words(0, 0, 1, 2)
        load_x_words(2, 4)
        load_w_words(0, 0, 2, 3)
        load_x_scales(2, 4)
        load_w_scales(0, 0, 2, 3)
        load_w_scales(0, 0, 3, 4)
        load_w_words(0, 0, 3, 4)
        load_x_words(4, G)
        load_x_scales(4, G)

        split_x(0, True)
        split_x(1, False)
        zero(wp[0], 4 * WS, G * WS)
        load_w_scales(0, 0, 4, 6)
        load_w_words(0, 0, 4, 5)
        load_w_words(0, 0, 5, 6)
        load_w_scales(0, 0, 6, G)
        load_w_words(0, 0, 6, 7)
        load_w_words(0, 0, 7, G)

        split_x(2, False)
        zero(wp[1], 0, G * WS // 2)
        split_x(3, False)
        zero(wp[1], G * WS // 2, G * WS)
        load_quad(2, 1)
        split_x(4, False)
        split_x(5, False)
        split_x(6, False)
        split_x(7, False)

        for i in range(WARM):
            nc.tensor.matmul(out=banks[7][:], lhsT=zeros[:, 0:P], rhs=zeros[:], start=True, stop=True)

        for c0 in range(0, QB, 2):
            for half in range(2):
                for c in (c0, c0 + 1):
                    for par in range(2):
                        mm(banks[2 * c + half], 0, par, half, 0, c, par == 0, False)
        for g in range(1, G):
            for half in range(2):
                for par in range(2):
                    for c in range(QB):
                        mm(banks[2 * c + half], g, par, half, 0, c, False, g == G - 1 and par == 1)
        for c in range(QB):
            for half in range(2):
                keys_out(banks[2 * c + half], c * NB, half, True, nc.sync)

        load_quad(3, 0)

        nxt = 0
        for quad, slot in ((2, 1), (3, 0)):
            for c in range(QB):
                for half in range(2):
                    be = banks[nxt % 8]
                    bo = banks[(nxt + 1) % 8]
                    nxt += 2
                    for g in range(G):
                        mm(be, g, 0, half, slot, c, g == 0, g == G - 1)
                    for g in range(G):
                        mm(bo, g, 1, half, slot, c, g == 0, g == G - 1)
                    values_out(be, bo, (quad - 2) * WS + c * NB, half)
            if quad == 2:
                load_quad(1, 1)

        for c in range(QB):
            for half in range(2):
                if c == QB - 1 and half == 1:
                    continue
                bk = banks[nxt % 8]
                nxt += 1
                for g in range(G):
                    for par in range(2):
                        mm(bk, g, par, half, 1, c, g == 0 and par == 0, g == G - 1 and par == 1)
                keys_out(bk, WS + c * NB, half, True, nc.sync)
        for part in range(2):
            bk = banks[nxt % 8]
            nxt += 1
            for g in range(G):
                for par in range(2):
                    mm(bk, g, par, 1, 1, QB - 1, g == 0 and par == 0, g == G - 1 and par == 1, part * 256, 256)
            keys_out(bk, WS + (QB - 1) * NB + part * 256, 1, True, nc.sync, 256)
